import numpy as np
import ml_dtypes


BF16 = ml_dtypes.bfloat16


def bf(x):
    return np.asarray(x, np.float32).astype(BF16)


def f64(x):
    return np.asarray(x).astype(np.float64)


E2M1 = np.array([0.0, 0.5, 1.0, 1.5, 2.0, 3.0, 4.0, 6.0, -0.0, -0.5, -1.0, -1.5, -2.0, -3.0, -4.0, -6.0])


def pack_weight(w, fmt):
    k, n = w.shape
    w = f64(bf(w)).reshape(k // 32, 32, n)
    amax = np.abs(w).max(1)
    if fmt == "e4m3":
        byte = np.frexp(amax)[1] - 1 + 127 - 7
    else:
        mant, ex = np.frexp(amax / 6.0)
        byte = np.where(mant > 0.5, ex, ex - 1) + 127
    byte = np.clip(np.where(amax > 0, byte, 1), 1, 254)
    scaled = (w * np.exp2(127.0 - byte)[:, None, :]).reshape(k, n).astype(np.float32)
    by_word = np.ascontiguousarray(scaled.reshape(k // 512, 128, 4, n).transpose(0, 1, 3, 2))
    if fmt == "e4m3":
        words = by_word.astype(ml_dtypes.float8_e4m3fn).view(np.uint8)
    else:
        c = by_word.astype(ml_dtypes.float4_e2m1fn).view(np.uint8) & 0xF
        words = c[..., 0::2] | (c[..., 1::2] << 4)
    return np.ascontiguousarray(words), np.ascontiguousarray(byte.astype(np.uint8).reshape(k // 512, 16, n))


def unpack_weight(words, scales, fmt):
    g, p, n, _ = words.shape
    if fmt == "e4m3":
        vals = np.ascontiguousarray(words).view(ml_dtypes.float8_e4m3fn).astype(np.float64)
    else:
        nib = np.empty((g, p, n, 4), np.uint8)
        nib[..., 0::2] = words & 0xF
        nib[..., 1::2] = words >> 4
        vals = E2M1[nib]
    vals = vals * np.repeat(np.exp2(scales.astype(np.float64) - 127.0), 8, axis=1)[..., None]
    return vals.transpose(0, 1, 3, 2).reshape(g * 512, n)

def pack4(w):
    words, scales = pack_weight(w, "e2m1")
    return words.reshape(words.shape[0], 128, -1), scales


def unpack4(words, scales):
    return unpack_weight(words.reshape(words.shape[0], 128, -1, 2), scales, "e2m1")


def kspread(k):
    return np.exp2(np.repeat(np.random.randint(-6, 7, k // 32), 32).astype(np.float64))


B, T, D, H = 1, 512, 1024, 16
KV = H // 2
DH = D // H


def rope(u):
    inv_freq = 1.0 / (10000.0 ** (np.arange(0, DH, 2) / DH))
    freqs = np.arange(T)[:, None] * inv_freq[None, :]
    sin = np.sin(freqs)[None, :, None, :]
    cos = np.cos(freqs)[None, :, None, :]
    u1, u2 = u[..., ::2], u[..., 1::2]
    even = u1 * cos - u2 * sin
    odd = u1 * sin + u2 * cos
    return np.stack([even, odd], axis=-1).reshape(u.shape)


def setup_inputs():
    s = kspread(D)
    x = np.random.standard_normal((B, T, D)) * s
    x_words, x_scales = pack4(x.reshape(B * T, D).T)
    Wq_words, Wq_scales = pack4(np.random.standard_normal((D, H * DH)) / np.sqrt(D) / s[:, None])
    bq = bf(np.random.standard_normal(H * DH) * 0.1)
    Wkv_words, Wkv_scales = pack4(np.random.standard_normal((D, 2 * KV * DH)) / np.sqrt(D) / s[:, None])
    bkv = bf(np.random.standard_normal(2 * KV * DH) * 0.1)
    return {"x_words": x_words,
            "x_scales": x_scales,
            "Wq_words": Wq_words,
            "Wq_scales": Wq_scales,
            "bq": bq,
            "Wkv_words": Wkv_words,
            "Wkv_scales": Wkv_scales,
            "bkv": bkv}


def reference(x_words, x_scales, Wq_words, Wq_scales, bq, Wkv_words, Wkv_scales, bkv):
    xq = unpack4(x_words, x_scales).T.reshape(B, T, D)
    q = ((xq @ unpack4(Wq_words, Wq_scales)) + f64(bq)).reshape(B, T, H, DH)
    kv = ((xq @ unpack4(Wkv_words, Wkv_scales)) + f64(bkv)).reshape(B, T, 2 * KV, DH)
    k, v = kv[:, :, :KV, :], kv[:, :, KV:, :]
    q = rope(q)
    k = rope(k)
    return q.transpose(0, 2, 1, 3), k.transpose(0, 2, 1, 3), v.transpose(0, 2, 1, 3)

@@ -1,0 +1,218 @@
+import math
+from contextlib import ExitStack
+
+import concourse.mybir as mybir
+from concourse.masks import make_identity
+
+F32 = mybir.dt.float32
+BF16 = mybir.dt.bfloat16
+I32 = mybir.dt.int32
+U8 = mybir.dt.uint8
+FP4X4 = mybir.dt.float4_e2m1fn_x4
+ALU = mybir.AluOpType
+ACT = mybir.ActivationFunctionType
+
+P = 128
+T = 512
+D = 1024
+G = D // 512
+NQ = 1024
+NKV = 1024
+DH = 64
+TB = T // P
+PAIRS = DH // 2
+
+FLOPS = 2 * T * D * (NQ + NKV)
+
+
+def tile_attention_pa_kernel(tc, x_words, x_scales, Wq_words, Wq_scales, bq, Wkv_words, Wkv_scales, bkv, out_0, out_1, out_2):
+    nc = tc.nc
+    with ExitStack() as ctx:
+        keep = ctx.enter_context(tc.tile_pool(name="keep", bufs=1))
+        work = ctx.enter_context(tc.tile_pool(name="work", bufs=3))
+        outs = ctx.enter_context(tc.tile_pool(name="outs", bufs=16))
+        ps_mx = ctx.enter_context(tc.psum_pool(name="ps_mx", bufs=5))
+        ps_tr = ctx.enter_context(tc.psum_pool(name="ps_tr", bufs=3))
+        ctx.enter_context(tc.manual_schedule())
+
+        x_codes = keep.tile([P, G, 2 * T], U8, name="x_codes", align_bytes=64)
+        x_plane = keep.tile([P, G, T], U8, name="x_plane", align_bytes=64)
+        v_codes = keep.tile([P, G, 2 * 512], U8, name="v_codes", align_bytes=64)
+        k_codes = keep.tile([P, G, 2 * 512], U8, name="k_codes", align_bytes=64)
+        kv_plane = keep.tile([P, G, NKV], U8, name="kv_plane", align_bytes=64)
+        q_codes = [keep.tile([P, G, 2 * 512], U8, name="q_codes%d" % i, align_bytes=64) for i in range(2)]
+        q_plane = keep.tile([P, G, NQ], U8, name="q_plane", align_bytes=64)
+
+        bias_rows = keep.tile([P, P], BF16, name="bias_rows")
+        cidx = keep.tile([P, 1], I32, name="cidx")
+        jrow = keep.tile([P, PAIRS], F32, name="jrow")
+        trow = keep.tile([P, T], F32, name="trow")
+        ident = keep.tile([P, P], F32, name="ident")
+        ident_bf = keep.tile([P, P], BF16, name="ident_bf")
+        swap = keep.tile([P, P], F32, name="swap")
+        jint = keep.tile([P, 1], I32, name="jint")
+        jcol = keep.tile([P, 1], F32, name="jcol")
+        par = keep.tile([P, 1], I32, name="par")
+        sgn = keep.tile([P, 1], F32, name="sgn")
+        one = keep.tile([P, 1], F32, name="one")
+        freq = keep.tile([P, PAIRS], F32, name="freq")
+        sel = keep.tile([P, PAIRS], F32, name="sel")
+        fcol = keep.tile([P, 1], F32, name="fcol")
+        turns = keep.tile([P, T], F32, name="turns")
+        whole = keep.tile([P, T], I32, name="whole")
+        frac = keep.tile([P, T], F32, name="frac")
+        afrac = keep.tile([P, T], F32, name="afrac")
+        cos_t = keep.tile([P, T], F32, name="cos_t")
+        sin_t = keep.tile([P, T], F32, name="sin_t")
+        warm = keep.tile([P, 1], F32, name="warm")
+        bcol = keep.tile([P, 16], F32, name="bcol")
+        vbias = keep.tile([P, 512], F32, name="vbias")
+
+        def load_codes(tile, words, lo, n):
+            nc.sync.dma_start(out=tile[:].bitcast(I32), in_=words[:, :, lo : lo + n].rearrange("g p n -> p g n").bitcast(I32))
+
+        def load_scales(plane, scales):
+            for q in range(4):
+                nc.sync.dma_start(
+                    out=plane[32 * q : 32 * q + 4, :, :].bitcast(I32),
+                    in_=scales[:, 4 * q : 4 * q + 4, :].rearrange("g r n -> r g n").bitcast(I32),
+                )
+
+        nc.vector.memset(x_plane[:].bitcast(I32), 0)
+        nc.vector.memset(kv_plane[:].bitcast(I32), 0)
+        load_codes(x_codes, x_words, 0, 2 * T)
+        load_codes(v_codes, Wkv_words, 1024, 1024)
+        load_scales(x_plane, x_scales)
+        load_scales(kv_plane, Wkv_scales)
+        load_codes(k_codes, Wkv_words, 0, 1024)
+
+        nc.gpsimd.memset(bias_rows[:].bitcast(I32), 0)
+        nc.gpsimd.dma_start(out=bias_rows[0:8, :], in_=bq.rearrange("(u c) -> u c", c=P))
+        nc.gpsimd.dma_start(out=bias_rows[8:16, :], in_=bkv.rearrange("(u c) -> u c", c=P))
+        nc.gpsimd.iota(cidx[:], pattern=[[0, 1]], base=0, channel_multiplier=1)
+        nc.gpsimd.iota(jrow[:], pattern=[[1, PAIRS]], base=0, channel_multiplier=0, allow_small_or_imprecise_dtypes=True)
+        nc.gpsimd.iota(trow[:], pattern=[[1, TB], [TB, P]], base=0, channel_multiplier=0, allow_small_or_imprecise_dtypes=True)
+        make_identity(nc, ident[:])
+
+        nc.vector.memset(one[:], 1.0)
+        nc.scalar.activation(out=warm[:], in_=one[:], func=ACT.Sin)
+        nc.vector.tensor_scalar(out=freq[:, 0:1], in0=one[:], scalar1=0.5 / math.pi, scalar2=None, op0=ALU.mult)
+        width = 1
+        while width < PAIRS:
+            nc.vector.tensor_scalar(out=freq[:, width : 2 * width], in0=freq[:, 0:width], scalar1=10000.0 ** (-2.0 * width / DH), scalar2=None, op0=ALU.mult)
+            width *= 2
+        nc.vector.tensor_scalar(out=jint[:], in0=cidx[:], scalar1=1, scalar2=PAIRS - 1, op0=ALU.logical_shift_right, op1=ALU.bitwise_and)
+        nc.vector.tensor_copy(out=jcol[:], in_=jint[:])
+        nc.vector.scalar_tensor_tensor(out=sel[:], in0=jrow[:], scalar=jcol[:], in1=freq[:], op0=ALU.is_equal, op1=ALU.mult, accum_out=fcol[:])
+        nc.vector.tensor_scalar(out=par[:], in0=cidx[:], scalar1=1, scalar2=1, op0=ALU.bitwise_and, op1=ALU.bitwise_and)
+        nc.vector.tensor_scalar(out=sgn[:], in0=par[:], scalar1=-4.0 * math.pi, scalar2=2.0 * math.pi, op0=ALU.mult, op1=ALU.add)
+        nc.vector.tensor_scalar(out=turns[:], in0=trow[:], scalar1=fcol[:], scalar2=None, op0=ALU.mult)
+        nc.vector.tensor_copy(out=whole[:], in_=turns[:])
+        nc.vector.tensor_tensor(out=frac[:], in0=turns[:], in1=whole[:], op=ALU.subtract)
+        nc.vector.memset(q_plane[:].bitcast(I32), 0)
+        load_codes(q_codes[0], Wq_words, 0, 1024)
+        load_scales(q_plane, Wq_scales)
+        load_codes(q_codes[1], Wq_words, 1024, 1024)
+        nc.scalar.copy(out=ident_bf[:], in_=ident[:])
+        nc.scalar.activation(out=afrac[:], in_=frac[:], func=ACT.Abs)
+        nc.scalar.activation(out=cos_t[:], in_=afrac[:], func=ACT.Sin, bias=0.5 * math.pi, scale=-2.0 * math.pi)
+        nc.scalar.activation(out=sin_t[:], in_=frac[:], func=ACT.Sin, scale=sgn[:])
+        pairs_i = ident[:].rearrange("p (j e) -> p j e", e=2)
+        pairs_s = swap[:].rearrange("p (j e) -> p j e", e=2)
+        nc.vector.tensor_copy(out=pairs_s[:, :, 0:1], in_=pairs_i[:, :, 1:2])
+        nc.vector.tensor_copy(out=pairs_s[:, :, 1:2], in_=pairs_i[:, :, 0:1])
+
+        ps_b = ps_tr.tile([P, 512], F32, name="tr")
+        nc.tensor.matmul(out=ps_b[:, 0:16], lhsT=bias_rows[:], rhs=ident_bf[:, 0:16], start=True, stop=True)
+        nc.scalar.copy(out=bcol[:], in_=ps_b[:, 0:16])
+        ps_v = ps_tr.tile([P, 512], F32, name="tr")
+        for u in range(4):
+            nc.tensor.matmul(out=ps_v[:, P * u : P * (u + 1)], lhsT=ident_bf[:, 12 + u : 13 + u].to_broadcast([P, P]), rhs=bias_rows[:], start=True, stop=True)
+        nc.scalar.copy(out=vbias[:], in_=ps_v[:])
+
+        for tb in range(TB):
+            acc = ps_mx.tile([P, 512], F32, name="mx")
+            for g in range(G):
+                nc.tensor.matmul_mx(
+                    out=acc[:],
+                    lhsT=x_codes[:, g, 256 * tb : 256 * (tb + 1)].bitcast(FP4X4),
+                    lhsT_scale=x_plane[:, g, P * tb : P * (tb + 1)],
+                    rhs=v_codes[:, g, :].bitcast(FP4X4),
+                    rhs_scale=kv_plane[:, g, 512:1024],
+                    start=(g == 0),
+                    stop=(g == G - 1),
+                )
+            v_out = outs.tile([P, 512], F32, name="out")
+            nc.vector.tensor_tensor(out=v_out[:], in0=acc[:], in1=vbias[:], op=ALU.add)
+            nc.sync.dma_start(
+                out=out_2[0, :, P * tb : P * (tb + 1), :].rearrange("h p d -> p h d"),
+                in_=v_out[:].rearrange("p (h d) -> p h d", d=DH),
+            )
+
+        units = []
+        for i in range(4):
+            units.append((k_codes, i, kv_plane, i, 8 + i, out_1, i))
+        for i in range(8):
+            units.append((q_codes[i // 4], i % 4, q_plane, i, i, out_0, i))
+
+        accs = {}
+
+        def project(n):
+            codes, ci, plane, pi, bi, out, oi = units[n]
+            acc = ps_mx.tile([P, 512], F32, name="mx")
+            for g in range(G):
+                nc.tensor.matmul_mx(
+                    out=acc[:],
+                    lhsT=codes[:, g, 256 * ci : 256 * (ci + 1)].bitcast(FP4X4),
+                    lhsT_scale=plane[:, g, P * pi : P * (pi + 1)],
+                    rhs=x_codes[:, g, :].bitcast(FP4X4),
+                    rhs_scale=x_plane[:, g, :],
+                    start=(g == 0),
+                    stop=(g == G - 1),
+                )
+            accs[n] = acc
+
+        rot = {}
+
+        def rotate(n):
+            bi = units[n][4]
+            acc = accs[n][:].rearrange("c (p b) -> c b p", b=TB)
+            m1 = work.tile([P, T], F32, name="m1")
+            m2 = work.tile([P, T], F32, name="m2")
+            for m, table in ((m1, cos_t), (m2, sin_t)):
+                nc.vector.scalar_tensor_tensor(
+                    out=m[:].rearrange("c (b p) -> c b p", b=TB),
+                    in0=acc,
+                    scalar=bcol[:, bi : bi + 1],
+                    in1=table[:].rearrange("c (b p) -> c b p", b=TB),
+                    op0=ALU.add,
+                    op1=ALU.mult,
+                )
+            rot[n] = (m1, m2)
+
+        def finish(n):
+            out, oi = units[n][5:]
+            m1, m2 = rot[n]
+            tr = ps_tr.tile([P, 512], F32, name="tr")
+            for b in range(TB):
+                cols = slice(P * b, P * (b + 1))
+                nc.tensor.matmul(out=tr[:, cols], lhsT=m1[:, cols], rhs=ident[:], start=True, stop=False, is_transpose=True)
+                nc.tensor.matmul(out=tr[:, cols], lhsT=m2[:, cols], rhs=swap[:], start=False, stop=True, is_transpose=True)
+            res = outs.tile([P, 512], F32, name="out")
+            nc.scalar.copy(
+                out=res[:].rearrange("p (h b d) -> p h b d", h=2, b=TB),
+                in_=tr[:].rearrange("p (b h d) -> p h b d", h=2, b=TB),
+            )
+            nc.sync.dma_start(
+                out=out[0, 2 * oi : 2 * oi + 2, :, :].rearrange("h (p b) d -> p h (b d)", b=TB),
+                in_=res[:].rearrange("p (h n) -> p h n", h=2),
+            )
+
+        count = len(units)
+        ahead = 2
+        for n in range(count + ahead):
+            if n < count:
+                project(n)
+                rotate(n)
+            if n >= ahead:
+                finish(n - ahead)

@@ -2,7 +2,6 @@ import math
 from contextlib import ExitStack
 
 import concourse.mybir as mybir
-from concourse.masks import make_identity
 
 F32 = mybir.dt.float32
 BF16 = mybir.dt.bfloat16
@@ -16,183 +15,196 @@ P = 128
 T = 512
 D = 1024
 G = D // 512
-NQ = 1024
-NKV = 1024
+N = 1024
 DH = 64
 TB = T // P
 PAIRS = DH // 2
+HALF = 512
+WARM_UP = 10
 
-FLOPS = 2 * T * D * (NQ + NKV)
+FLOPS = 2 * T * D * (N + N)
+
+
+def i32(ap):
+    return ap.bitcast(I32)
 
 
 def tile_attention_pa_kernel(tc, x_words, x_scales, Wq_words, Wq_scales, bq, Wkv_words, Wkv_scales, bkv, out_0, out_1, out_2):
     nc = tc.nc
     with ExitStack() as ctx:
         keep = ctx.enter_context(tc.tile_pool(name="keep", bufs=1))
-        work = ctx.enter_context(tc.tile_pool(name="work", bufs=3))
+        work = ctx.enter_context(tc.tile_pool(name="work", bufs=4))
         outs = ctx.enter_context(tc.tile_pool(name="outs", bufs=16))
-        ps_mx = ctx.enter_context(tc.psum_pool(name="ps_mx", bufs=5))
-        ps_tr = ctx.enter_context(tc.psum_pool(name="ps_tr", bufs=3))
+        ps_mx = ctx.enter_context(tc.psum_pool(name="ps_mx", bufs=4))
+        ps_tr = ctx.enter_context(tc.psum_pool(name="ps_tr", bufs=4))
         ctx.enter_context(tc.manual_schedule())
 
-        x_codes = keep.tile([P, G, 2 * T], U8, name="x_codes", align_bytes=64)
+        x_codes = [keep.tile([P, 2 * T], U8, name="x_codes%d" % g, align_bytes=64) for g in range(G)]
         x_plane = keep.tile([P, G, T], U8, name="x_plane", align_bytes=64)
-        v_codes = keep.tile([P, G, 2 * 512], U8, name="v_codes", align_bytes=64)
-        k_codes = keep.tile([P, G, 2 * 512], U8, name="k_codes", align_bytes=64)
-        kv_plane = keep.tile([P, G, NKV], U8, name="kv_plane", align_bytes=64)
-        q_codes = [keep.tile([P, G, 2 * 512], U8, name="q_codes%d" % i, align_bytes=64) for i in range(2)]
-        q_plane = keep.tile([P, G, NQ], U8, name="q_plane", align_bytes=64)
+        k_codes = [keep.tile([P, 2 * HALF], U8, name="k_codes%d" % g, align_bytes=64) for g in range(G)]
+        v_codes = [keep.tile([P, 2 * HALF], U8, name="v_codes%d" % g, align_bytes=64) for g in range(G)]
+        kv_plane = keep.tile([P, G, N], U8, name="kv_plane", align_bytes=64)
+        q_codes = keep.tile([P, G, 2 * N], U8, name="q_codes", align_bytes=64)
+        q_plane = keep.tile([P, G, N], U8, name="q_plane", align_bytes=64)
 
-        bias_rows = keep.tile([P, P], BF16, name="bias_rows")
-        cidx = keep.tile([P, 1], I32, name="cidx")
-        jrow = keep.tile([P, PAIRS], F32, name="jrow")
+        kv_rows = keep.tile([P, P], BF16, name="kv_rows")
+        q_rows = keep.tile([P, P], BF16, name="q_rows")
+        kv_col = keep.tile([P, 8], F32, name="kv_col")
+        q_col = keep.tile([P, 8], F32, name="q_col")
+        v_bias = keep.tile([P, HALF], F32, name="v_bias")
+
+        one = keep.tile([P, 1], F32, name="one")
+        warm = keep.tile([P, 1], F32, name="warm")
+        part = keep.tile([P, 1], I32, name="part")
+        part_f = keep.tile([P, 1], F32, name="part_f")
+        row = keep.tile([P, P], F32, name="row")
         trow = keep.tile([P, T], F32, name="trow")
-        ident = keep.tile([P, P], F32, name="ident")
         ident_bf = keep.tile([P, P], BF16, name="ident_bf")
+        ident = keep.tile([P, P], F32, name="ident")
         swap = keep.tile([P, P], F32, name="swap")
         jint = keep.tile([P, 1], I32, name="jint")
         jcol = keep.tile([P, 1], F32, name="jcol")
-        par = keep.tile([P, 1], I32, name="par")
-        sgn = keep.tile([P, 1], F32, name="sgn")
-        one = keep.tile([P, 1], F32, name="one")
+        odd = keep.tile([P, 1], I32, name="odd")
+        sign = keep.tile([P, 1], F32, name="sign")
         freq = keep.tile([P, PAIRS], F32, name="freq")
-        sel = keep.tile([P, PAIRS], F32, name="sel")
+        own = keep.tile([P, PAIRS], F32, name="own")
         fcol = keep.tile([P, 1], F32, name="fcol")
         turns = keep.tile([P, T], F32, name="turns")
         whole = keep.tile([P, T], I32, name="whole")
         frac = keep.tile([P, T], F32, name="frac")
-        afrac = keep.tile([P, T], F32, name="afrac")
-        cos_t = keep.tile([P, T], F32, name="cos_t")
-        sin_t = keep.tile([P, T], F32, name="sin_t")
-        warm = keep.tile([P, 1], F32, name="warm")
-        bcol = keep.tile([P, 16], F32, name="bcol")
-        vbias = keep.tile([P, 512], F32, name="vbias")
-
-        def load_codes(tile, words, lo, n):
-            nc.sync.dma_start(out=tile[:].bitcast(I32), in_=words[:, :, lo : lo + n].rearrange("g p n -> p g n").bitcast(I32))
+        dist = keep.tile([P, T], F32, name="dist")
+        cos = keep.tile([P, T], F32, name="cos")
+        sin = keep.tile([P, T], F32, name="sin")
 
         def load_scales(plane, scales):
             for q in range(4):
                 nc.sync.dma_start(
-                    out=plane[32 * q : 32 * q + 4, :, :].bitcast(I32),
-                    in_=scales[:, 4 * q : 4 * q + 4, :].rearrange("g r n -> r g n").bitcast(I32),
+                    out=i32(plane[32 * q : 32 * q + 4, :, :]),
+                    in_=i32(scales[:, 4 * q : 4 * q + 4, :].rearrange("g r n -> r g n")),
                 )
 
-        nc.vector.memset(x_plane[:].bitcast(I32), 0)
-        nc.vector.memset(kv_plane[:].bitcast(I32), 0)
-        load_codes(x_codes, x_words, 0, 2 * T)
-        load_codes(v_codes, Wkv_words, 1024, 1024)
+        nc.vector.memset(one[:], 1.0)
+        nc.vector.memset(i32(kv_rows[:]), 0)
+        nc.vector.memset(i32(x_plane[:]), 0)
+        nc.vector.memset(i32(kv_plane[:]), 0)
+        nc.vector.memset(i32(q_rows[:]), 0)
+        nc.sync.dma_start(out=i32(x_codes[0][:]), in_=i32(x_words[0, :, :]))
+        nc.sync.dma_start(out=i32(k_codes[0][:]), in_=i32(Wkv_words[0, :, 0 : 2 * HALF]))
         load_scales(x_plane, x_scales)
         load_scales(kv_plane, Wkv_scales)
-        load_codes(k_codes, Wkv_words, 0, 1024)
+        nc.sync.dma_start(out=i32(x_codes[1][:]), in_=i32(x_words[1, :, :]))
+        nc.sync.dma_start(out=i32(k_codes[1][:]), in_=i32(Wkv_words[1, :, 0 : 2 * HALF]))
+        for g in range(G):
+            nc.sync.dma_start(out=i32(v_codes[g][:]), in_=i32(Wkv_words[g, :, 2 * HALF : 4 * HALF]))
 
-        nc.gpsimd.memset(bias_rows[:].bitcast(I32), 0)
-        nc.gpsimd.dma_start(out=bias_rows[0:8, :], in_=bq.rearrange("(u c) -> u c", c=P))
-        nc.gpsimd.dma_start(out=bias_rows[8:16, :], in_=bkv.rearrange("(u c) -> u c", c=P))
-        nc.gpsimd.iota(cidx[:], pattern=[[0, 1]], base=0, channel_multiplier=1)
-        nc.gpsimd.iota(jrow[:], pattern=[[1, PAIRS]], base=0, channel_multiplier=0, allow_small_or_imprecise_dtypes=True)
+        nc.gpsimd.iota(row[:], pattern=[[1, P]], base=0, channel_multiplier=0, allow_small_or_imprecise_dtypes=True)
+        nc.gpsimd.iota(part_f[:], pattern=[[0, 1]], base=0, channel_multiplier=1, allow_small_or_imprecise_dtypes=True)
+        nc.gpsimd.iota(part[:], pattern=[[0, 1]], base=0, channel_multiplier=1)
+        nc.gpsimd.dma_start(out=kv_rows[0:8, :], in_=bkv.rearrange("(u c) -> u c", c=P))
         nc.gpsimd.iota(trow[:], pattern=[[1, TB], [TB, P]], base=0, channel_multiplier=0, allow_small_or_imprecise_dtypes=True)
-        make_identity(nc, ident[:])
+        nc.gpsimd.dma_start(out=q_rows[0:8, :], in_=bq.rearrange("(u c) -> u c", c=P))
+        nc.gpsimd.memset(i32(q_plane[:]), 0)
+        load_scales(q_plane, Wq_scales)
+        nc.sync.dma_start(out=i32(q_codes[:]), in_=i32(Wq_words.rearrange("g p n -> p g n")))
 
-        nc.vector.memset(one[:], 1.0)
         nc.scalar.activation(out=warm[:], in_=one[:], func=ACT.Sin)
-        nc.vector.tensor_scalar(out=freq[:, 0:1], in0=one[:], scalar1=0.5 / math.pi, scalar2=None, op0=ALU.mult)
-        width = 1
-        while width < PAIRS:
-            nc.vector.tensor_scalar(out=freq[:, width : 2 * width], in0=freq[:, 0:width], scalar1=10000.0 ** (-2.0 * width / DH), scalar2=None, op0=ALU.mult)
-            width *= 2
-        nc.vector.tensor_scalar(out=jint[:], in0=cidx[:], scalar1=1, scalar2=PAIRS - 1, op0=ALU.logical_shift_right, op1=ALU.bitwise_and)
+
+        nc.vector.tensor_scalar(out=ident_bf[:], in0=row[:], scalar1=part_f[:], scalar2=None, op0=ALU.is_equal)
+        for j in range(4):
+            nc.vector.tensor_scalar(out=freq[:, j : j + 1], in0=one[:], scalar1=0.5 / math.pi * 10000.0 ** (-2.0 * j / DH), scalar2=None, op0=ALU.mult)
+        for j in (4, 8, 16):
+            nc.vector.tensor_scalar(out=freq[:, j : 2 * j], in0=freq[:, 0:j], scalar1=10000.0 ** (-2.0 * j / DH), scalar2=None, op0=ALU.mult)
+        nc.vector.tensor_scalar(out=jint[:], in0=part[:], scalar1=1, scalar2=PAIRS - 1, op0=ALU.logical_shift_right, op1=ALU.bitwise_and)
+        nc.vector.tensor_scalar(out=odd[:], in0=part[:], scalar1=1, scalar2=1, op0=ALU.bitwise_and, op1=ALU.bitwise_and)
         nc.vector.tensor_copy(out=jcol[:], in_=jint[:])
-        nc.vector.scalar_tensor_tensor(out=sel[:], in0=jrow[:], scalar=jcol[:], in1=freq[:], op0=ALU.is_equal, op1=ALU.mult, accum_out=fcol[:])
-        nc.vector.tensor_scalar(out=par[:], in0=cidx[:], scalar1=1, scalar2=1, op0=ALU.bitwise_and, op1=ALU.bitwise_and)
-        nc.vector.tensor_scalar(out=sgn[:], in0=par[:], scalar1=-4.0 * math.pi, scalar2=2.0 * math.pi, op0=ALU.mult, op1=ALU.add)
+        nc.vector.tensor_scalar(out=sign[:], in0=odd[:], scalar1=-4.0 * math.pi, scalar2=2.0 * math.pi, op0=ALU.mult, op1=ALU.add)
+        nc.vector.scalar_tensor_tensor(out=own[:], in0=row[:, 0:PAIRS], scalar=jcol[:], in1=freq[:], op0=ALU.is_equal, op1=ALU.mult, accum_out=fcol[:])
         nc.vector.tensor_scalar(out=turns[:], in0=trow[:], scalar1=fcol[:], scalar2=None, op0=ALU.mult)
         nc.vector.tensor_copy(out=whole[:], in_=turns[:])
         nc.vector.tensor_tensor(out=frac[:], in0=turns[:], in1=whole[:], op=ALU.subtract)
-        nc.vector.memset(q_plane[:].bitcast(I32), 0)
-        load_codes(q_codes[0], Wq_words, 0, 1024)
-        load_scales(q_plane, Wq_scales)
-        load_codes(q_codes[1], Wq_words, 1024, 1024)
-        nc.scalar.copy(out=ident_bf[:], in_=ident[:])
-        nc.scalar.activation(out=afrac[:], in_=frac[:], func=ACT.Abs)
-        nc.scalar.activation(out=cos_t[:], in_=afrac[:], func=ACT.Sin, bias=0.5 * math.pi, scale=-2.0 * math.pi)
-        nc.scalar.activation(out=sin_t[:], in_=frac[:], func=ACT.Sin, scale=sgn[:])
-        pairs_i = ident[:].rearrange("p (j e) -> p j e", e=2)
-        pairs_s = swap[:].rearrange("p (j e) -> p j e", e=2)
-        nc.vector.tensor_copy(out=pairs_s[:, :, 0:1], in_=pairs_i[:, :, 1:2])
-        nc.vector.tensor_copy(out=pairs_s[:, :, 1:2], in_=pairs_i[:, :, 0:1])
+        nc.vector.scalar_tensor_tensor(out=dist[:], in0=frac[:], scalar=-1.0, in1=frac[:], op0=ALU.mult, op1=ALU.max)
+        nc.vector.tensor_scalar(out=ident[:], in0=row[:], scalar1=part_f[:], scalar2=None, op0=ALU.is_equal)
+        pair = "p (n e) -> p n e"
+        nc.vector.tensor_copy(out=swap[:].rearrange(pair, e=2), in_=ident[:].rearrange(pair, e=2)[:, :, ::-1])
 
-        ps_b = ps_tr.tile([P, 512], F32, name="tr")
-        nc.tensor.matmul(out=ps_b[:, 0:16], lhsT=bias_rows[:], rhs=ident_bf[:, 0:16], start=True, stop=True)
-        nc.scalar.copy(out=bcol[:], in_=ps_b[:, 0:16])
-        ps_v = ps_tr.tile([P, 512], F32, name="tr")
-        for u in range(4):
-            nc.tensor.matmul(out=ps_v[:, P * u : P * (u + 1)], lhsT=ident_bf[:, 12 + u : 13 + u].to_broadcast([P, P]), rhs=bias_rows[:], start=True, stop=True)
-        nc.scalar.copy(out=vbias[:], in_=ps_v[:])
+        nc.scalar.activation(out=sin[:], in_=frac[:], func=ACT.Sin, scale=sign[:])
+        nc.scalar.activation(out=cos[:], in_=dist[:], func=ACT.Sin, bias=0.5 * math.pi, scale=-2.0 * math.pi)
 
-        for tb in range(TB):
-            acc = ps_mx.tile([P, 512], F32, name="mx")
-            for g in range(G):
-                nc.tensor.matmul_mx(
-                    out=acc[:],
-                    lhsT=x_codes[:, g, 256 * tb : 256 * (tb + 1)].bitcast(FP4X4),
-                    lhsT_scale=x_plane[:, g, P * tb : P * (tb + 1)],
-                    rhs=v_codes[:, g, :].bitcast(FP4X4),
-                    rhs_scale=kv_plane[:, g, 512:1024],
-                    start=(g == 0),
-                    stop=(g == G - 1),
-                )
-            v_out = outs.tile([P, 512], F32, name="out")
-            nc.vector.tensor_tensor(out=v_out[:], in0=acc[:], in1=vbias[:], op=ALU.add)
-            nc.sync.dma_start(
-                out=out_2[0, :, P * tb : P * (tb + 1), :].rearrange("h p d -> p h d"),
-                in_=v_out[:].rearrange("p (h d) -> p h d", d=DH),
+        bank = ps_tr.tile([P, 512], F32, name="tr")
+        for i in range(WARM_UP):
+            nc.tensor.matmul(
+                out=bank[:].rearrange("p (r c) -> p r c", c=P),
+                lhsT=ident_bf[:],
+                rhs=ident_bf[:].rearrange("p (r c) -> p r c", r=1).to_broadcast([P, 4, P]),
+                start=True,
+                stop=True,
             )
 
-        units = []
-        for i in range(4):
-            units.append((k_codes, i, kv_plane, i, 8 + i, out_1, i))
-        for i in range(8):
-            units.append((q_codes[i // 4], i % 4, q_plane, i, i, out_0, i))
+        def bias_columns(cols, rows):
+            bank = ps_tr.tile([P, 512], F32, name="tr")
+            nc.tensor.matmul(out=bank[:, 0:8], lhsT=rows[:], rhs=ident_bf[:, 0:8], start=True, stop=True)
+            nc.scalar.copy(out=cols[:], in_=bank[:, 0:8])
 
-        accs = {}
+        bias_columns(kv_col, kv_rows)
 
-        def project(n):
-            codes, ci, plane, pi, bi, out, oi = units[n]
-            acc = ps_mx.tile([P, 512], F32, name="mx")
+        def project(acc, stationary, s_plane, moving, m_plane):
             for g in range(G):
                 nc.tensor.matmul_mx(
                     out=acc[:],
-                    lhsT=codes[:, g, 256 * ci : 256 * (ci + 1)].bitcast(FP4X4),
-                    lhsT_scale=plane[:, g, P * pi : P * (pi + 1)],
-                    rhs=x_codes[:, g, :].bitcast(FP4X4),
-                    rhs_scale=x_plane[:, g, :],
+                    lhsT=stationary[g].bitcast(FP4X4),
+                    lhsT_scale=s_plane[g],
+                    rhs=moving[g].bitcast(FP4X4),
+                    rhs_scale=m_plane[g],
                     start=(g == 0),
                     stop=(g == G - 1),
                 )
-            accs[n] = acc
 
-        rot = {}
+        def value(b):
+            acc = ps_mx.tile([P, 512], F32, name="mx")
+            project(
+                acc,
+                [x_codes[g][:, 2 * P * b : 2 * P * (b + 1)] for g in range(G)],
+                [x_plane[:, g, P * b : P * (b + 1)] for g in range(G)],
+                [v_codes[g][:] for g in range(G)],
+                [kv_plane[:, g, HALF:N] for g in range(G)],
+            )
+            res = outs.tile([P, 512], F32, name="out")
+            nc.vector.tensor_tensor(out=res[:], in0=acc[:], in1=v_bias[:], op=ALU.add)
+            nc.sync.dma_start(
+                out=out_2[0, :, P * b : P * (b + 1), :].rearrange("h p d -> p h d"),
+                in_=res[:].rearrange("p (h d) -> p h d", d=DH),
+            )
+
+        def unit(codes, plane, i, bias, out):
+            return (
+                [codes[g][:, 2 * P * i : 2 * P * (i + 1)] for g in range(G)],
+                [plane[:, g, P * i : P * (i + 1)] for g in range(G)],
+                bias[:, i : i + 1],
+                out[0, 2 * i : 2 * i + 2, :, :],
+            )
+
+        units = [unit(k_codes, kv_plane, i, kv_col, out_1) for i in range(4)]
+        units += [unit([q_codes[:, g, :] for g in range(G)], q_plane, i, q_col, out_0) for i in range(8)]
 
         def rotate(n):
-            bi = units[n][4]
-            acc = accs[n][:].rearrange("c (p b) -> c b p", b=TB)
+            codes, scales, bias, out = units[n]
+            acc = ps_mx.tile([P, 512], F32, name="mx")
+            project(acc, codes, scales, [x_codes[g][:] for g in range(G)], [x_plane[:, g, :] for g in range(G)])
             m1 = work.tile([P, T], F32, name="m1")
             m2 = work.tile([P, T], F32, name="m2")
-            for m, table in ((m1, cos_t), (m2, sin_t)):
+            for m, table in ((m1, cos), (m2, sin)):
                 nc.vector.scalar_tensor_tensor(
                     out=m[:].rearrange("c (b p) -> c b p", b=TB),
-                    in0=acc,
-                    scalar=bcol[:, bi : bi + 1],
+                    in0=acc[:].rearrange("c (p b) -> c b p", b=TB),
+                    scalar=bias,
                     in1=table[:].rearrange("c (b p) -> c b p", b=TB),
                     op0=ALU.add,
                     op1=ALU.mult,
                 )
-            rot[n] = (m1, m2)
+            return m1, m2
 
-        def finish(n):
-            out, oi = units[n][5:]
-            m1, m2 = rot[n]
+        def turn(n, m1, m2):
+            out = units[n][3]
             tr = ps_tr.tile([P, 512], F32, name="tr")
             for b in range(TB):
                 cols = slice(P * b, P * (b + 1))
@@ -204,15 +216,24 @@ def tile_attention_pa_kernel(tc, x_words, x_scales, Wq_words, Wq_scales, bq, Wkv
                 in_=tr[:].rearrange("p (b h d) -> p h b d", h=2, b=TB),
             )
             nc.sync.dma_start(
-                out=out[0, 2 * oi : 2 * oi + 2, :, :].rearrange("h (p b) d -> p h (b d)", b=TB),
+                out=out.rearrange("h (p b) d -> p h (b d)", b=TB),
                 in_=res[:].rearrange("p (h n) -> p h n", h=2),
             )
 
-        count = len(units)
-        ahead = 2
-        for n in range(count + ahead):
-            if n < count:
-                project(n)
-                rotate(n)
-            if n >= ahead:
-                finish(n - ahead)
+        products = {}
+        for n in (0, 1):
+            products[n] = rotate(n)
+        bank = ps_tr.tile([P, 512], F32, name="tr")
+        for u in range(4):
+            nc.tensor.matmul(out=bank[:, P * u : P * (u + 1)], lhsT=ident_bf[:, 4 + u : 5 + u].to_broadcast([P, P]), rhs=kv_rows[:], start=True, stop=True)
+        nc.scalar.copy(out=v_bias[:], in_=bank[:])
+        bias_columns(q_col, q_rows)
+        for s in range(1, 6):
+            if s <= TB:
+                value(s - 1)
+            for n in (2 * s, 2 * s + 1):
+                products[n] = rotate(n)
+            for n in (2 * s - 2, 2 * s - 1):
+                turn(n, *products[n])
+        for n in (10, 11):
+            turn(n, *products[n])

@@ -146,6 +146,10 @@ def tile_attention_pa_kernel(tc, x_words, x_scales, Wq_words, Wq_scales, bq, Wkv
             nc.scalar.copy(out=cols[:], in_=bank[:, 0:8])
 
         bias_columns(kv_col, kv_rows)
+        bank = ps_tr.tile([P, 512], F32, name="tr")
+        for u in range(4):
+            nc.tensor.matmul(out=bank[:, P * u : P * (u + 1)], lhsT=ident_bf[:, 4 + u : 5 + u].to_broadcast([P, P]), rhs=kv_rows[:], start=True, stop=True)
+        nc.scalar.copy(out=v_bias[:], in_=bank[:])
 
         def project(acc, stationary, s_plane, moving, m_plane):
             for g in range(G):
@@ -187,7 +191,7 @@ def tile_attention_pa_kernel(tc, x_words, x_scales, Wq_words, Wq_scales, bq, Wkv
         units += [unit([q_codes[:, g, :] for g in range(G)], q_plane, i, q_col, out_0) for i in range(8)]
 
         def rotate(n):
-            codes, scales, bias, out = units[n]
+            codes, scales, bias = units[n][0:3]
             acc = ps_mx.tile([P, 512], F32, name="mx")
             project(acc, codes, scales, [x_codes[g][:] for g in range(G)], [x_plane[:, g, :] for g in range(G)])
             m1 = work.tile([P, T], F32, name="m1")
@@ -203,37 +207,34 @@ def tile_attention_pa_kernel(tc, x_words, x_scales, Wq_words, Wq_scales, bq, Wkv
                 )
             return m1, m2
 
-        def turn(n, m1, m2):
-            out = units[n][3]
-            tr = ps_tr.tile([P, 512], F32, name="tr")
-            for b in range(TB):
-                cols = slice(P * b, P * (b + 1))
-                nc.tensor.matmul(out=tr[:, cols], lhsT=m1[:, cols], rhs=ident[:], start=True, stop=False, is_transpose=True)
-                nc.tensor.matmul(out=tr[:, cols], lhsT=m2[:, cols], rhs=swap[:], start=False, stop=True, is_transpose=True)
+        def turn(n, m1, m2, copy_second=nc.scalar.copy):
+            halves = [ps_tr.tile([P, 256], F32, name="tr") for h in range(2)]
+            for i in range(2):
+                cols = slice(P * i, P * (i + 1))
+                for m, perm, first in ((m1, ident, True), (m2, swap, False)):
+                    for h in range(2):
+                        b = 2 * h + i
+                        nc.tensor.matmul(out=halves[h][:, cols], lhsT=m[:, P * b : P * (b + 1)], rhs=perm[:], start=first, stop=not first, is_transpose=True)
             res = outs.tile([P, 512], F32, name="out")
-            nc.scalar.copy(
-                out=res[:].rearrange("p (h b d) -> p h b d", h=2, b=TB),
-                in_=tr[:].rearrange("p (b h d) -> p h b d", h=2, b=TB),
-            )
+            by_head = res[:].rearrange("p (h b d) -> p h b d", h=2, b=TB)
+            for h, copy in ((0, nc.scalar.copy), (1, copy_second)):
+                copy(out=by_head[:, :, 2 * h : 2 * h + 2, :], in_=halves[h][:].rearrange("p (b h d) -> p h b d", h=2, b=2))
             nc.sync.dma_start(
-                out=out.rearrange("h (p b) d -> p h (b d)", b=TB),
+                out=units[n][3].rearrange("h (p b) d -> p h (b d)", b=TB),
                 in_=res[:].rearrange("p (h n) -> p h n", h=2),
             )
 
         products = {}
         for n in (0, 1):
             products[n] = rotate(n)
-        bank = ps_tr.tile([P, 512], F32, name="tr")
-        for u in range(4):
-            nc.tensor.matmul(out=bank[:, P * u : P * (u + 1)], lhsT=ident_bf[:, 4 + u : 5 + u].to_broadcast([P, P]), rhs=kv_rows[:], start=True, stop=True)
-        nc.scalar.copy(out=v_bias[:], in_=bank[:])
+            value(n)
         bias_columns(q_col, q_rows)
         for s in range(1, 6):
-            if s <= TB:
-                value(s - 1)
+            if s in (2, 3):
+                value(s)
             for n in (2 * s, 2 * s + 1):
                 products[n] = rotate(n)
             for n in (2 * s - 2, 2 * s - 1):
                 turn(n, *products[n])
-        for n in (10, 11):
-            turn(n, *products[n])
+        turn(10, *products[10])
+        turn(11, *products[11], copy_second=nc.vector.tensor_copy)

import math
from contextlib import ExitStack

import concourse.mybir as mybir

F32 = mybir.dt.float32
BF16 = mybir.dt.bfloat16
I32 = mybir.dt.int32
U8 = mybir.dt.uint8
FP4X4 = mybir.dt.float4_e2m1fn_x4
ALU = mybir.AluOpType
ACT = mybir.ActivationFunctionType

P = 128
T = 512
D = 1024
G = D // 512
N = 1024
DH = 64
TB = T // P
PAIRS = DH // 2
HALF = 512
WARM_UP = 10

FLOPS = 2 * T * D * (N + N)


def i32(ap):
    return ap.bitcast(I32)


def tile_attention_pa_kernel(tc, x_words, x_scales, Wq_words, Wq_scales, bq, Wkv_words, Wkv_scales, bkv, out_0, out_1, out_2):
    nc = tc.nc
    with ExitStack() as ctx:
        keep = ctx.enter_context(tc.tile_pool(name="keep", bufs=1))
        work = ctx.enter_context(tc.tile_pool(name="work", bufs=4))
        outs = ctx.enter_context(tc.tile_pool(name="outs", bufs=16))
        ps_mx = ctx.enter_context(tc.psum_pool(name="ps_mx", bufs=4))
        ps_tr = ctx.enter_context(tc.psum_pool(name="ps_tr", bufs=4))
        ctx.enter_context(tc.manual_schedule())

        x_codes = [keep.tile([P, 2 * T], U8, name="x_codes%d" % g, align_bytes=64) for g in range(G)]
        x_plane = keep.tile([P, G, T], U8, name="x_plane", align_bytes=64)
        k_codes = [keep.tile([P, 2 * HALF], U8, name="k_codes%d" % g, align_bytes=64) for g in range(G)]
        v_codes = [keep.tile([P, 2 * HALF], U8, name="v_codes%d" % g, align_bytes=64) for g in range(G)]
        kv_plane = keep.tile([P, G, N], U8, name="kv_plane", align_bytes=64)
        q_codes = keep.tile([P, G, 2 * N], U8, name="q_codes", align_bytes=64)
        q_plane = keep.tile([P, G, N], U8, name="q_plane", align_bytes=64)

        kv_rows = keep.tile([P, P], BF16, name="kv_rows")
        q_rows = keep.tile([P, P], BF16, name="q_rows")
        kv_col = keep.tile([P, 8], F32, name="kv_col")
        q_col = keep.tile([P, 8], F32, name="q_col")
        v_bias = keep.tile([P, HALF], F32, name="v_bias")

        one = keep.tile([P, 1], F32, name="one")
        warm = keep.tile([P, 1], F32, name="warm")
        part = keep.tile([P, 1], I32, name="part")
        part_f = keep.tile([P, 1], F32, name="part_f")
        row = keep.tile([P, P], F32, name="row")
        trow = keep.tile([P, T], F32, name="trow")
        ident_bf = keep.tile([P, P], BF16, name="ident_bf")
        ident = keep.tile([P, P], F32, name="ident")
        swap = keep.tile([P, P], F32, name="swap")
        jint = keep.tile([P, 1], I32, name="jint")
        jcol = keep.tile([P, 1], F32, name="jcol")
        odd = keep.tile([P, 1], I32, name="odd")
        sign = keep.tile([P, 1], F32, name="sign")
        freq = keep.tile([P, PAIRS], F32, name="freq")
        own = keep.tile([P, PAIRS], F32, name="own")
        fcol = keep.tile([P, 1], F32, name="fcol")
        turns = keep.tile([P, T], F32, name="turns")
        whole = keep.tile([P, T], I32, name="whole")
        frac = keep.tile([P, T], F32, name="frac")
        dist = keep.tile([P, T], F32, name="dist")
        cos = keep.tile([P, T], F32, name="cos")
        sin = keep.tile([P, T], F32, name="sin")

        def load_scales(plane, scales):
            for q in range(4):
                nc.sync.dma_start(
                    out=i32(plane[32 * q : 32 * q + 4, :, :]),
                    in_=i32(scales[:, 4 * q : 4 * q + 4, :].rearrange("g r n -> r g n")),
                )

        nc.vector.memset(one[:], 1.0)
        nc.vector.memset(i32(kv_rows[:]), 0)
        nc.vector.memset(i32(x_plane[:]), 0)
        nc.vector.memset(i32(kv_plane[:]), 0)
        nc.vector.memset(i32(q_rows[:]), 0)
        nc.sync.dma_start(out=i32(x_codes[0][:]), in_=i32(x_words[0, :, :]))
        nc.sync.dma_start(out=i32(k_codes[0][:]), in_=i32(Wkv_words[0, :, 0 : 2 * HALF]))
        load_scales(x_plane, x_scales)
        load_scales(kv_plane, Wkv_scales)
        nc.sync.dma_start(out=i32(x_codes[1][:]), in_=i32(x_words[1, :, :]))
        nc.sync.dma_start(out=i32(k_codes[1][:]), in_=i32(Wkv_words[1, :, 0 : 2 * HALF]))
        for g in range(G):
            nc.sync.dma_start(out=i32(v_codes[g][:]), in_=i32(Wkv_words[g, :, 2 * HALF : 4 * HALF]))

        nc.gpsimd.iota(row[:], pattern=[[1, P]], base=0, channel_multiplier=0, allow_small_or_imprecise_dtypes=True)
        nc.gpsimd.iota(part_f[:], pattern=[[0, 1]], base=0, channel_multiplier=1, allow_small_or_imprecise_dtypes=True)
        nc.gpsimd.iota(part[:], pattern=[[0, 1]], base=0, channel_multiplier=1)
        nc.gpsimd.dma_start(out=kv_rows[0:8, :], in_=bkv.rearrange("(u c) -> u c", c=P))
        nc.gpsimd.iota(trow[:], pattern=[[1, TB], [TB, P]], base=0, channel_multiplier=0, allow_small_or_imprecise_dtypes=True)
        nc.gpsimd.dma_start(out=q_rows[0:8, :], in_=bq.rearrange("(u c) -> u c", c=P))
        nc.gpsimd.memset(i32(q_plane[:]), 0)
        load_scales(q_plane, Wq_scales)
        nc.sync.dma_start(out=i32(q_codes[:]), in_=i32(Wq_words.rearrange("g p n -> p g n")))

        nc.scalar.activation(out=warm[:], in_=one[:], func=ACT.Sin)

        nc.vector.tensor_scalar(out=ident_bf[:], in0=row[:], scalar1=part_f[:], scalar2=None, op0=ALU.is_equal)
        for j in range(4):
            nc.vector.tensor_scalar(out=freq[:, j : j + 1], in0=one[:], scalar1=0.5 / math.pi * 10000.0 ** (-2.0 * j / DH), scalar2=None, op0=ALU.mult)
        for j in (4, 8, 16):
            nc.vector.tensor_scalar(out=freq[:, j : 2 * j], in0=freq[:, 0:j], scalar1=10000.0 ** (-2.0 * j / DH), scalar2=None, op0=ALU.mult)
        nc.vector.tensor_scalar(out=jint[:], in0=part[:], scalar1=1, scalar2=PAIRS - 1, op0=ALU.logical_shift_right, op1=ALU.bitwise_and)
        nc.vector.tensor_scalar(out=odd[:], in0=part[:], scalar1=1, scalar2=1, op0=ALU.bitwise_and, op1=ALU.bitwise_and)
        nc.vector.tensor_copy(out=jcol[:], in_=jint[:])
        nc.vector.tensor_scalar(out=sign[:], in0=odd[:], scalar1=-4.0 * math.pi, scalar2=2.0 * math.pi, op0=ALU.mult, op1=ALU.add)
        nc.vector.scalar_tensor_tensor(out=own[:], in0=row[:, 0:PAIRS], scalar=jcol[:], in1=freq[:], op0=ALU.is_equal, op1=ALU.mult, accum_out=fcol[:])
        nc.vector.tensor_scalar(out=turns[:], in0=trow[:], scalar1=fcol[:], scalar2=None, op0=ALU.mult)
        nc.vector.tensor_copy(out=whole[:], in_=turns[:])
        nc.vector.tensor_tensor(out=frac[:], in0=turns[:], in1=whole[:], op=ALU.subtract)
        nc.vector.scalar_tensor_tensor(out=dist[:], in0=frac[:], scalar=-1.0, in1=frac[:], op0=ALU.mult, op1=ALU.max)
        nc.vector.tensor_scalar(out=ident[:], in0=row[:], scalar1=part_f[:], scalar2=None, op0=ALU.is_equal)
        pair = "p (n e) -> p n e"
        nc.vector.tensor_copy(out=swap[:].rearrange(pair, e=2), in_=ident[:].rearrange(pair, e=2)[:, :, ::-1])

        nc.scalar.activation(out=sin[:], in_=frac[:], func=ACT.Sin, scale=sign[:])
        nc.scalar.activation(out=cos[:], in_=dist[:], func=ACT.Sin, bias=0.5 * math.pi, scale=-2.0 * math.pi)

        bank = ps_tr.tile([P, 512], F32, name="tr")
        for i in range(WARM_UP):
            nc.tensor.matmul(
                out=bank[:].rearrange("p (r c) -> p r c", c=P),
                lhsT=ident_bf[:],
                rhs=ident_bf[:].rearrange("p (r c) -> p r c", r=1).to_broadcast([P, 4, P]),
                start=True,
                stop=True,
            )

        def bias_columns(cols, rows):
            bank = ps_tr.tile([P, 512], F32, name="tr")
            nc.tensor.matmul(out=bank[:, 0:8], lhsT=rows[:], rhs=ident_bf[:, 0:8], start=True, stop=True)
            nc.scalar.copy(out=cols[:], in_=bank[:, 0:8])

        bias_columns(kv_col, kv_rows)
        bank = ps_tr.tile([P, 512], F32, name="tr")
        for u in range(4):
            nc.tensor.matmul(out=bank[:, P * u : P * (u + 1)], lhsT=ident_bf[:, 4 + u : 5 + u].to_broadcast([P, P]), rhs=kv_rows[:], start=True, stop=True)
        nc.scalar.copy(out=v_bias[:], in_=bank[:])

        def project(acc, stationary, s_plane, moving, m_plane):
            for g in range(G):
                nc.tensor.matmul_mx(
                    out=acc[:],
                    lhsT=stationary[g].bitcast(FP4X4),
                    lhsT_scale=s_plane[g],
                    rhs=moving[g].bitcast(FP4X4),
                    rhs_scale=m_plane[g],
                    start=(g == 0),
                    stop=(g == G - 1),
                )

        def value(b):
            acc = ps_mx.tile([P, 512], F32, name="mx")
            project(
                acc,
                [x_codes[g][:, 2 * P * b : 2 * P * (b + 1)] for g in range(G)],
                [x_plane[:, g, P * b : P * (b + 1)] for g in range(G)],
                [v_codes[g][:] for g in range(G)],
                [kv_plane[:, g, HALF:N] for g in range(G)],
            )
            res = outs.tile([P, 512], F32, name="out")
            nc.vector.tensor_tensor(out=res[:], in0=acc[:], in1=v_bias[:], op=ALU.add)
            nc.sync.dma_start(
                out=out_2[0, :, P * b : P * (b + 1), :].rearrange("h p d -> p h d"),
                in_=res[:].rearrange("p (h d) -> p h d", d=DH),
            )

        def unit(codes, plane, i, bias, out):
            return (
                [codes[g][:, 2 * P * i : 2 * P * (i + 1)] for g in range(G)],
                [plane[:, g, P * i : P * (i + 1)] for g in range(G)],
                bias[:, i : i + 1],
                out[0, 2 * i : 2 * i + 2, :, :],
            )

        units = [unit(k_codes, kv_plane, i, kv_col, out_1) for i in range(4)]
        units += [unit([q_codes[:, g, :] for g in range(G)], q_plane, i, q_col, out_0) for i in range(8)]

        def rotate(n):
            codes, scales, bias = units[n][0:3]
            acc = ps_mx.tile([P, 512], F32, name="mx")
            project(acc, codes, scales, [x_codes[g][:] for g in range(G)], [x_plane[:, g, :] for g in range(G)])
            m1 = work.tile([P, T], F32, name="m1")
            m2 = work.tile([P, T], F32, name="m2")
            for m, table in ((m1, cos), (m2, sin)):
                nc.vector.scalar_tensor_tensor(
                    out=m[:].rearrange("c (b p) -> c b p", b=TB),
                    in0=acc[:].rearrange("c (p b) -> c b p", b=TB),
                    scalar=bias,
                    in1=table[:].rearrange("c (b p) -> c b p", b=TB),
                    op0=ALU.add,
                    op1=ALU.mult,
                )
            return m1, m2

        def turn(n, m1, m2, copy_second=nc.scalar.copy):
            halves = [ps_tr.tile([P, 256], F32, name="tr") for h in range(2)]
            for i in range(2):
                cols = slice(P * i, P * (i + 1))
                for m, perm, first in ((m1, ident, True), (m2, swap, False)):
                    for h in range(2):
                        b = 2 * h + i
                        nc.tensor.matmul(out=halves[h][:, cols], lhsT=m[:, P * b : P * (b + 1)], rhs=perm[:], start=first, stop=not first, is_transpose=True)
            res = outs.tile([P, 512], F32, name="out")
            by_head = res[:].rearrange("p (h b d) -> p h b d", h=2, b=TB)
            for h, copy in ((0, nc.scalar.copy), (1, copy_second)):
                copy(out=by_head[:, :, 2 * h : 2 * h + 2, :], in_=halves[h][:].rearrange("p (b h d) -> p h b d", h=2, b=2))
            nc.sync.dma_start(
                out=units[n][3].rearrange("h (p b) d -> p h (b d)", b=TB),
                in_=res[:].rearrange("p (h n) -> p h n", h=2),
            )

        products = {}
        for n in (0, 1):
            products[n] = rotate(n)
            value(n)
        bias_columns(q_col, q_rows)
        for s in range(1, 6):
            if s in (2, 3):
                value(s)
            for n in (2 * s, 2 * s + 1):
                products[n] = rotate(n)
            for n in (2 * s - 2, 2 * s - 1):
                turn(n, *products[n])
        turn(10, *products[10])
        turn(11, *products[11], copy_second=nc.vector.tensor_copy)
